import numpy as np
import ml_dtypes

BF16 = ml_dtypes.bfloat16


def bf(x):
    return np.asarray(x, np.float32).astype(BF16)


def f32(x):
    return np.asarray(x, np.float32)


def f64(x):
    return np.asarray(x).astype(np.float64)


def striped(idx):
    return np.tile(idx.reshape(-1, 16).T, (8, 1))


D, C, S, B, M, T, N = 128, 256, 2048, 16, 128, 4, 8192
SCALE = 0.6


def setup_inputs():
    return {"table": f32(SCALE * np.random.standard_normal((C, S))), "offs": striped(np.concatenate([np.random.permutation(S) for _ in range(T)]))}


def reference(table, offs):
    idx = offs[:16].T.reshape(-1)
    e = f64(table)[:, idx].reshape(C, T, B, M).sum(axis=1)
    a, v = e[:D], e[D:]
    u1 = a.sum(axis=2) / M
    z = (a * u1[:, :, None]).sum(axis=0)
    w = np.exp(z - z.max(axis=1, keepdims=True))
    p = w / w.sum(axis=1, keepdims=True)
    return u1 + (v * p[None, :, :]).sum(axis=2)

@@ -1,0 +1,94 @@
+import concourse.mybir as mybir
+
+F32 = mybir.dt.float32
+BF16 = mybir.dt.bfloat16
+U16 = mybir.dt.uint16
+ADD = mybir.AluOpType.add
+MULT = mybir.AluOpType.mult
+EXP = mybir.ActivationFunctionType.Exp
+X = mybir.AxisListType.X
+
+P = 128
+VOCAB = 2048
+STORIES = 16
+SENTENCES = 128
+WORDS = 4
+COLS = STORIES * SENTENCES
+BANK = 512
+
+FLOPS = 2 * 2 * P * COLS
+
+
+def tile_encodermemnn_kernel(tc, table, offs, out):
+    nc = tc.nc
+    with (
+        tc.tile_pool(name="held", bufs=1) as held,
+        tc.tile_pool(name="running", bufs=2) as running,
+        tc.psum_pool(name="psum", bufs=1) as psum,
+    ):
+        offsets = held.tile([P, WORDS * COLS // 16], U16, name="offsets")
+        nc.sync.dma_start(offsets[:], offs)
+        address_table = held.tile([P, VOCAB], F32, name="address_table")
+        nc.scalar.dma_start(address_table[:], table[0:P, :])
+        value_table = held.tile([P, VOCAB], F32, name="value_table")
+        nc.sync.dma_start(value_table[:], table[P : 2 * P, :])
+
+        ones = held.tile([P, P], BF16, name="ones")
+        nc.vector.memset(ones[:], 1.0)
+
+        def by_story(ap):
+            return ap.rearrange("p (b m) -> p b m", m=SENTENCES)
+
+        def sentence_sums(window, name):
+            sums = None
+            for t in range(WORDS):
+                words = window[:].indirect(offsets[:, t * COLS // 16 : (t + 1) * COLS // 16])
+                longer = running.tile([P, COLS], F32, name=name)
+                if t == 0:
+                    nc.vector.tensor_copy(longer[:], words)
+                else:
+                    nc.vector.tensor_tensor(longer[:], words, sums[:], ADD)
+                sums = longer
+            return sums
+
+        a = sentence_sums(address_table, "a")
+
+        u1 = held.tile([P, STORIES], F32, name="u1")
+        nc.vector.reduce_sum(u1[:], by_story(a[:]), axis=X)
+        nc.scalar.mul(u1[:], u1[:], 1.0 / SENTENCES)
+
+        products = held.tile([P, COLS], BF16, name="products")
+        nc.vector.tensor_tensor(
+            by_story(products[:]),
+            by_story(a[:]),
+            u1[:].unsqueeze(2).to_broadcast([P, STORIES, SENTENCES]),
+            MULT,
+        )
+        z = psum.tile([P, COLS], F32, name="z")
+        minus_max = held.tile([P, STORIES], F32, name="minus_max")
+        per_bank = BANK // SENTENCES
+        for k in range(COLS // BANK):
+            bank = slice(k * BANK, (k + 1) * BANK)
+            nc.tensor.matmul(z[:, bank], ones[:], products[:, bank], start=True, stop=True)
+            nc.vector.reduce_max(
+                minus_max[:, k * per_bank : (k + 1) * per_bank], by_story(z[:, bank]), axis=X, negate=True
+            )
+
+        w = held.tile([P, COLS], F32, name="w")
+        w_sum = held.tile([P, STORIES], F32, name="w_sum")
+        for b in range(STORIES):
+            story = slice(b * SENTENCES, (b + 1) * SENTENCES)
+            nc.scalar.activation(
+                w[:, story], z[:, story], EXP, bias=minus_max[:, b : b + 1], accum_out=w_sum[:, b : b + 1]
+            )
+        w_scale = held.tile([P, STORIES], F32, name="w_scale")
+        nc.vector.reciprocal(w_scale[:], w_sum[:])
+
+        v = sentence_sums(value_table, "v")
+
+        nc.vector.tensor_tensor(w[:], w[:], v[:], MULT)
+        result = held.tile([P, STORIES], F32, name="result")
+        nc.vector.reduce_sum(result[:], by_story(w[:]), axis=X)
+        nc.vector.tensor_tensor(result[:], result[:], w_scale[:], MULT)
+        nc.vector.tensor_tensor(result[:], result[:], u1[:], ADD)
+        nc.sync.dma_start(out, result[:])

@@ -1,10 +1,12 @@
 import concourse.mybir as mybir
+from concourse.masks import make_identity
 
 F32 = mybir.dt.float32
 BF16 = mybir.dt.bfloat16
 U16 = mybir.dt.uint16
 ADD = mybir.AluOpType.add
 MULT = mybir.AluOpType.mult
+COPY = mybir.ActivationFunctionType.Copy
 EXP = mybir.ActivationFunctionType.Exp
 X = mybir.AxisListType.X
 
@@ -14,6 +16,7 @@ STORIES = 16
 SENTENCES = 128
 WORDS = 4
 COLS = STORIES * SENTENCES
+HALF = COLS // 2
 BANK = 512
 
 FLOPS = 2 * 2 * P * COLS
@@ -23,72 +26,106 @@ def tile_encodermemnn_kernel(tc, table, offs, out):
     nc = tc.nc
     with (
         tc.tile_pool(name="held", bufs=1) as held,
-        tc.tile_pool(name="running", bufs=2) as running,
         tc.psum_pool(name="psum", bufs=1) as psum,
     ):
         offsets = held.tile([P, WORDS * COLS // 16], U16, name="offsets")
         nc.sync.dma_start(offsets[:], offs)
         address_table = held.tile([P, VOCAB], F32, name="address_table")
-        nc.scalar.dma_start(address_table[:], table[0:P, :])
+        nc.sync.dma_start(address_table[:], table[0:P, :])
         value_table = held.tile([P, VOCAB], F32, name="value_table")
         nc.sync.dma_start(value_table[:], table[P : 2 * P, :])
 
         ones = held.tile([P, P], BF16, name="ones")
-        nc.vector.memset(ones[:], 1.0)
+        nc.gpsimd.memset(ones[:], 1.0)
+        selector = held.tile([P, 2 * STORIES - 1], BF16, name="selector")
+        nc.gpsimd.memset(selector[:], 0.0)
+        nc.gpsimd.memset(selector[:, STORIES - 1 : STORIES], 1.0)
+        story_ones = held.tile([STORIES, P], F32, name="story_ones")
+        nc.gpsimd.memset(story_ones[:], 1.0)
+        story_identity = held.tile([STORIES, STORIES], F32, name="story_identity")
+        make_identity(nc, story_identity[:])
 
-        def by_story(ap):
-            return ap.rearrange("p (b m) -> p b m", m=SENTENCES)
+        def wide_tile(turn, dtype):
+            return held.tile([P, COLS], dtype, name=f"wide{turn}", tag=f"slot{turn % 3}")
 
-        def sentence_sums(window, name):
-            sums = None
-            for t in range(WORDS):
-                words = window[:].indirect(offsets[:, t * COLS // 16 : (t + 1) * COLS // 16])
-                longer = running.tile([P, COLS], F32, name=name)
-                if t == 0:
-                    nc.vector.tensor_copy(longer[:], words)
-                else:
-                    nc.vector.tensor_tensor(longer[:], words, sums[:], ADD)
-                sums = longer
-            return sums
+        def story(b):
+            return slice(b * SENTENCES, (b + 1) * SENTENCES)
 
-        a = sentence_sums(address_table, "a")
+        def add_words(window, t, first, width, sums, longer):
+            cols = slice(first, first + width)
+            entry = t * COLS + first
+            words = window[:].indirect(offsets[:, entry // 16 : (entry + width) // 16])
+            if t == 0:
+                nc.vector.tensor_copy(longer[:, cols], words)
+            else:
+                nc.vector.tensor_tensor(longer[:, cols], words, sums[:, cols], ADD)
+
+        a = None
+        for t in range(WORDS):
+            longer = wide_tile(t, F32)
+            for first in range(0, COLS, HALF):
+                add_words(address_table, t, first, HALF, a, longer)
+            a = longer
 
         u1 = held.tile([P, STORIES], F32, name="u1")
-        nc.vector.reduce_sum(u1[:], by_story(a[:]), axis=X)
-        nc.scalar.mul(u1[:], u1[:], 1.0 / SENTENCES)
-
-        products = held.tile([P, COLS], BF16, name="products")
-        nc.vector.tensor_tensor(
-            by_story(products[:]),
-            by_story(a[:]),
-            u1[:].unsqueeze(2).to_broadcast([P, STORIES, SENTENCES]),
-            MULT,
-        )
-        z = psum.tile([P, COLS], F32, name="z")
-        minus_max = held.tile([P, STORIES], F32, name="minus_max")
-        per_bank = BANK // SENTENCES
-        for k in range(COLS // BANK):
-            bank = slice(k * BANK, (k + 1) * BANK)
-            nc.tensor.matmul(z[:, bank], ones[:], products[:, bank], start=True, stop=True)
-            nc.vector.reduce_max(
-                minus_max[:, k * per_bank : (k + 1) * per_bank], by_story(z[:, bank]), axis=X, negate=True
+        unused = held.tile([P, SENTENCES], F32, name="unused")
+        products = wide_tile(WORDS, BF16)
+        for b in range(STORIES):
+            nc.scalar.activation(
+                unused[:], a[:, story(b)], COPY, scale=1.0 / SENTENCES, accum_out=u1[:, b : b + 1]
             )
+            nc.scalar.activation(products[:, story(b)], a[:, story(b)], COPY, scale=u1[:, b : b + 1])
+
+        z_by_story = psum.tile([STORIES, SENTENCES], F32, name="z_by_story")
+        for b in range(STORIES):
+            nc.tensor.matmul(
+                z_by_story[:],
+                selector[:, STORIES - 1 - b : 2 * STORIES - 1 - b],
+                products[:, story(b)],
+                start=(b == 0),
+                stop=(b == STORIES - 1),
+            )
+        z = psum.tile([P, COLS], F32, name="z")
+        for first in range(0, COLS, BANK):
+            bank = slice(first, first + BANK)
+            nc.tensor.matmul(z[:, bank], ones[:], products[:, bank], start=True, stop=True)
+
+        minus_max = held.tile([STORIES, 1], F32, name="minus_max")
+        nc.vector.reduce_max(minus_max[:], z_by_story[:], axis=X, negate=True)
+        diagonal = held.tile([STORIES, STORIES], F32, name="diagonal")
+        nc.scalar.activation(diagonal[:], story_identity[:], COPY, scale=minus_max[:, 0:1])
+        shift_psum = psum.tile([P, STORIES], F32, name="shift_psum")
+        nc.tensor.matmul(shift_psum[:], story_ones[:], diagonal[:], start=True, stop=True)
+        shift = held.tile([P, STORIES], F32, name="shift")
+        nc.scalar.copy(shift[:], shift_psum[:])
 
         w = held.tile([P, COLS], F32, name="w")
         w_sum = held.tile([P, STORIES], F32, name="w_sum")
         for b in range(STORIES):
-            story = slice(b * SENTENCES, (b + 1) * SENTENCES)
             nc.scalar.activation(
-                w[:, story], z[:, story], EXP, bias=minus_max[:, b : b + 1], accum_out=w_sum[:, b : b + 1]
+                w[:, story(b)], z[:, story(b)], EXP, bias=shift[:, b : b + 1], accum_out=w_sum[:, b : b + 1]
             )
         w_scale = held.tile([P, STORIES], F32, name="w_scale")
         nc.vector.reciprocal(w_scale[:], w_sum[:])
 
-        v = sentence_sums(value_table, "v")
+        v = None
+        for t in range(WORDS - 1):
+            longer = wide_tile(WORDS + 1 + t, F32)
+            for first in range(0, COLS, HALF):
+                add_words(value_table, t, first, HALF, v, longer)
+            v = longer
 
-        nc.vector.tensor_tensor(w[:], w[:], v[:], MULT)
+        longer = wide_tile(2 * WORDS, F32)
+        weighted = held.tile([P, COLS], F32, name="weighted")
+        hop2 = held.tile([P, STORIES], F32, name="hop2")
+        for first in range(0, COLS, BANK):
+            piece = slice(first, first + BANK)
+            add_words(value_table, WORDS - 1, first, BANK, v, longer)
+            nc.vector.tensor_tensor(weighted[:, piece], longer[:, piece], w[:, piece], MULT)
+            for b in range(first // SENTENCES, (first + BANK) // SENTENCES):
+                nc.scalar.activation(unused[:], weighted[:, story(b)], COPY, accum_out=hop2[:, b : b + 1])
+
         result = held.tile([P, STORIES], F32, name="result")
-        nc.vector.reduce_sum(result[:], by_story(w[:]), axis=X)
-        nc.vector.tensor_tensor(result[:], result[:], w_scale[:], MULT)
+        nc.vector.tensor_tensor(result[:], hop2[:], w_scale[:], MULT)
         nc.vector.tensor_tensor(result[:], result[:], u1[:], ADD)
         nc.sync.dma_start(out, result[:])

@@ -26,6 +26,8 @@ def tile_encodermemnn_kernel(tc, table, offs, out):
     nc = tc.nc
     with (
         tc.tile_pool(name="held", bufs=1) as held,
+        tc.tile_pool(name="a_passes", bufs=3) as a_passes,
+        tc.tile_pool(name="pieces", bufs=2) as pieces,
         tc.psum_pool(name="psum", bufs=1) as psum,
     ):
         offsets = held.tile([P, WORDS * COLS // 16], U16, name="offsets")
@@ -45,31 +47,34 @@ def tile_encodermemnn_kernel(tc, table, offs, out):
         story_identity = held.tile([STORIES, STORIES], F32, name="story_identity")
         make_identity(nc, story_identity[:])
 
-        def wide_tile(turn, dtype):
-            return held.tile([P, COLS], dtype, name=f"wide{turn}", tag=f"slot{turn % 3}")
+        def late_tile(turn, dtype):
+            return held.tile([P, COLS], dtype, name=f"late{turn}", tag=f"slot{turn % 3}")
 
         def story(b):
             return slice(b * SENTENCES, (b + 1) * SENTENCES)
 
-        def add_words(window, t, first, width, sums, longer):
-            cols = slice(first, first + width)
+        def add_words(window, t, first, shorter, longer):
             entry = t * COLS + first
-            words = window[:].indirect(offsets[:, entry // 16 : (entry + width) // 16])
+            words = window[:].indirect(offsets[:, entry // 16 : (entry + longer.shape[1]) // 16])
             if t == 0:
-                nc.vector.tensor_copy(longer[:, cols], words)
+                nc.vector.tensor_copy(longer, words)
             else:
-                nc.vector.tensor_tensor(longer[:, cols], words, sums[:, cols], ADD)
+                nc.vector.tensor_tensor(longer, words, shorter, ADD)
+
+        def pass_by_halves(window, t, sums, longer):
+            for first in range(0, COLS, HALF):
+                half = slice(first, first + HALF)
+                add_words(window, t, first, None if t == 0 else sums[:, half], longer[:, half])
 
         a = None
         for t in range(WORDS):
-            longer = wide_tile(t, F32)
-            for first in range(0, COLS, HALF):
-                add_words(address_table, t, first, HALF, a, longer)
+            longer = a_passes.tile([P, COLS], F32, name="a")
+            pass_by_halves(address_table, t, a, longer)
             a = longer
 
         u1 = held.tile([P, STORIES], F32, name="u1")
         unused = held.tile([P, SENTENCES], F32, name="unused")
-        products = wide_tile(WORDS, BF16)
+        products = late_tile(0, BF16)
         for b in range(STORIES):
             nc.scalar.activation(
                 unused[:], a[:, story(b)], COPY, scale=1.0 / SENTENCES, accum_out=u1[:, b : b + 1]
@@ -110,18 +115,17 @@ def tile_encodermemnn_kernel(tc, table, offs, out):
 
         v = None
         for t in range(WORDS - 1):
-            longer = wide_tile(WORDS + 1 + t, F32)
-            for first in range(0, COLS, HALF):
-                add_words(value_table, t, first, HALF, v, longer)
+            longer = late_tile(1 + t, F32)
+            pass_by_halves(value_table, t, v, longer)
             v = longer
 
-        longer = wide_tile(2 * WORDS, F32)
         weighted = held.tile([P, COLS], F32, name="weighted")
         hop2 = held.tile([P, STORIES], F32, name="hop2")
         for first in range(0, COLS, BANK):
             piece = slice(first, first + BANK)
-            add_words(value_table, WORDS - 1, first, BANK, v, longer)
-            nc.vector.tensor_tensor(weighted[:, piece], longer[:, piece], w[:, piece], MULT)
+            v_piece = pieces.tile([P, BANK], F32, name="v_piece")
+            add_words(value_table, WORDS - 1, first, v[:, piece], v_piece[:])
+            nc.vector.tensor_tensor(weighted[:, piece], v_piece[:], w[:, piece], MULT)
             for b in range(first // SENTENCES, (first + BANK) // SENTENCES):
                 nc.scalar.activation(unused[:], weighted[:, story(b)], COPY, accum_out=hop2[:, b : b + 1])
 

@@ -120,16 +120,24 @@ def tile_encodermemnn_kernel(tc, table, offs, out):
             v = longer
 
         weighted = held.tile([P, COLS], F32, name="weighted")
-        hop2 = held.tile([P, STORIES], F32, name="hop2")
+        hop2 = held.tile([P, STORIES, 2], F32, name="hop2")
         for first in range(0, COLS, BANK):
             piece = slice(first, first + BANK)
             v_piece = pieces.tile([P, BANK], F32, name="v_piece")
             add_words(value_table, WORDS - 1, first, v[:, piece], v_piece[:])
             nc.vector.tensor_tensor(weighted[:, piece], v_piece[:], w[:, piece], MULT)
-            for b in range(first // SENTENCES, (first + BANK) // SENTENCES):
-                nc.scalar.activation(unused[:], weighted[:, story(b)], COPY, accum_out=hop2[:, b : b + 1])
+            stories = range(first // SENTENCES, (first + BANK) // SENTENCES)
+            if first + BANK < COLS:
+                for b in stories:
+                    nc.scalar.activation(unused[:], weighted[:, story(b)], COPY, accum_out=hop2[:, b, 0:1])
+            else:
+                nc.vector.reduce_sum(
+                    hop2[:, stories[0] : STORIES, 0],
+                    weighted[:, piece].rearrange("p (b m) -> p b m", m=SENTENCES),
+                    axis=X,
+                )
 
         result = held.tile([P, STORIES], F32, name="result")
-        nc.vector.tensor_tensor(result[:], hop2[:], w_scale[:], MULT)
+        nc.vector.tensor_tensor(result[:], hop2[:, :, 0], w_scale[:], MULT)
         nc.vector.tensor_tensor(result[:], result[:], u1[:], ADD)
         nc.sync.dma_start(out, result[:])

@@ -47,6 +47,10 @@ def tile_encodermemnn_kernel(tc, table, offs, out):
         story_identity = held.tile([STORIES, STORIES], F32, name="story_identity")
         make_identity(nc, story_identity[:])
 
+        warm = held.tile([P, 1], F32, name="warm")
+        nc.gpsimd.memset(warm[:], 0.0)
+        nc.scalar.activation(warm[:], warm[:], EXP)
+
         def late_tile(turn, dtype):
             return held.tile([P, COLS], dtype, name=f"late{turn}", tag=f"slot{turn % 3}")
 

@@ -34,8 +34,6 @@ def tile_encodermemnn_kernel(tc, table, offs, out):
         nc.sync.dma_start(offsets[:], offs)
         address_table = held.tile([P, VOCAB], F32, name="address_table")
         nc.sync.dma_start(address_table[:], table[0:P, :])
-        value_table = held.tile([P, VOCAB], F32, name="value_table")
-        nc.sync.dma_start(value_table[:], table[P : 2 * P, :])
 
         ones = held.tile([P, P], BF16, name="ones")
         nc.gpsimd.memset(ones[:], 1.0)
@@ -47,9 +45,11 @@ def tile_encodermemnn_kernel(tc, table, offs, out):
         story_identity = held.tile([STORIES, STORIES], F32, name="story_identity")
         make_identity(nc, story_identity[:])
 
-        warm = held.tile([P, 1], F32, name="warm")
+        warm = held.tile([P, 1], F32, name="warm", tag="value_table")
         nc.gpsimd.memset(warm[:], 0.0)
         nc.scalar.activation(warm[:], warm[:], EXP)
+        value_table = held.tile([P, VOCAB], F32, name="value_table", tag="value_table")
+        nc.sync.dma_start(value_table[:], table[P : 2 * P, :])
 
         def late_tile(turn, dtype):
             return held.tile([P, COLS], dtype, name=f"late{turn}", tag=f"slot{turn % 3}")

import concourse.mybir as mybir
from concourse.masks import make_identity

F32 = mybir.dt.float32
BF16 = mybir.dt.bfloat16
U16 = mybir.dt.uint16
ADD = mybir.AluOpType.add
MULT = mybir.AluOpType.mult
COPY = mybir.ActivationFunctionType.Copy
EXP = mybir.ActivationFunctionType.Exp
X = mybir.AxisListType.X

P = 128
VOCAB = 2048
STORIES = 16
SENTENCES = 128
WORDS = 4
COLS = STORIES * SENTENCES
HALF = COLS // 2
BANK = 512

FLOPS = 2 * 2 * P * COLS


def tile_encodermemnn_kernel(tc, table, offs, out):
    nc = tc.nc
    with (
        tc.tile_pool(name="held", bufs=1) as held,
        tc.tile_pool(name="a_passes", bufs=3) as a_passes,
        tc.tile_pool(name="pieces", bufs=2) as pieces,
        tc.psum_pool(name="psum", bufs=1) as psum,
    ):
        offsets = held.tile([P, WORDS * COLS // 16], U16, name="offsets")
        nc.sync.dma_start(offsets[:], offs)
        address_table = held.tile([P, VOCAB], F32, name="address_table")
        nc.sync.dma_start(address_table[:], table[0:P, :])

        ones = held.tile([P, P], BF16, name="ones")
        nc.gpsimd.memset(ones[:], 1.0)
        selector = held.tile([P, 2 * STORIES - 1], BF16, name="selector")
        nc.gpsimd.memset(selector[:], 0.0)
        nc.gpsimd.memset(selector[:, STORIES - 1 : STORIES], 1.0)
        story_ones = held.tile([STORIES, P], F32, name="story_ones")
        nc.gpsimd.memset(story_ones[:], 1.0)
        story_identity = held.tile([STORIES, STORIES], F32, name="story_identity")
        make_identity(nc, story_identity[:])

        warm = held.tile([P, 1], F32, name="warm", tag="value_table")
        nc.gpsimd.memset(warm[:], 0.0)
        nc.scalar.activation(warm[:], warm[:], EXP)
        value_table = held.tile([P, VOCAB], F32, name="value_table", tag="value_table")
        nc.sync.dma_start(value_table[:], table[P : 2 * P, :])

        def late_tile(turn, dtype):
            return held.tile([P, COLS], dtype, name=f"late{turn}", tag=f"slot{turn % 3}")

        def story(b):
            return slice(b * SENTENCES, (b + 1) * SENTENCES)

        def add_words(window, t, first, shorter, longer):
            entry = t * COLS + first
            words = window[:].indirect(offsets[:, entry // 16 : (entry + longer.shape[1]) // 16])
            if t == 0:
                nc.vector.tensor_copy(longer, words)
            else:
                nc.vector.tensor_tensor(longer, words, shorter, ADD)

        def pass_by_halves(window, t, sums, longer):
            for first in range(0, COLS, HALF):
                half = slice(first, first + HALF)
                add_words(window, t, first, None if t == 0 else sums[:, half], longer[:, half])

        a = None
        for t in range(WORDS):
            longer = a_passes.tile([P, COLS], F32, name="a")
            pass_by_halves(address_table, t, a, longer)
            a = longer

        u1 = held.tile([P, STORIES], F32, name="u1")
        unused = held.tile([P, SENTENCES], F32, name="unused")
        products = late_tile(0, BF16)
        for b in range(STORIES):
            nc.scalar.activation(
                unused[:], a[:, story(b)], COPY, scale=1.0 / SENTENCES, accum_out=u1[:, b : b + 1]
            )
            nc.scalar.activation(products[:, story(b)], a[:, story(b)], COPY, scale=u1[:, b : b + 1])

        z_by_story = psum.tile([STORIES, SENTENCES], F32, name="z_by_story")
        for b in range(STORIES):
            nc.tensor.matmul(
                z_by_story[:],
                selector[:, STORIES - 1 - b : 2 * STORIES - 1 - b],
                products[:, story(b)],
                start=(b == 0),
                stop=(b == STORIES - 1),
            )
        z = psum.tile([P, COLS], F32, name="z")
        for first in range(0, COLS, BANK):
            bank = slice(first, first + BANK)
            nc.tensor.matmul(z[:, bank], ones[:], products[:, bank], start=True, stop=True)

        minus_max = held.tile([STORIES, 1], F32, name="minus_max")
        nc.vector.reduce_max(minus_max[:], z_by_story[:], axis=X, negate=True)
        diagonal = held.tile([STORIES, STORIES], F32, name="diagonal")
        nc.scalar.activation(diagonal[:], story_identity[:], COPY, scale=minus_max[:, 0:1])
        shift_psum = psum.tile([P, STORIES], F32, name="shift_psum")
        nc.tensor.matmul(shift_psum[:], story_ones[:], diagonal[:], start=True, stop=True)
        shift = held.tile([P, STORIES], F32, name="shift")
        nc.scalar.copy(shift[:], shift_psum[:])

        w = held.tile([P, COLS], F32, name="w")
        w_sum = held.tile([P, STORIES], F32, name="w_sum")
        for b in range(STORIES):
            nc.scalar.activation(
                w[:, story(b)], z[:, story(b)], EXP, bias=shift[:, b : b + 1], accum_out=w_sum[:, b : b + 1]
            )
        w_scale = held.tile([P, STORIES], F32, name="w_scale")
        nc.vector.reciprocal(w_scale[:], w_sum[:])

        v = None
        for t in range(WORDS - 1):
            longer = late_tile(1 + t, F32)
            pass_by_halves(value_table, t, v, longer)
            v = longer

        weighted = held.tile([P, COLS], F32, name="weighted")
        hop2 = held.tile([P, STORIES, 2], F32, name="hop2")
        for first in range(0, COLS, BANK):
            piece = slice(first, first + BANK)
            v_piece = pieces.tile([P, BANK], F32, name="v_piece")
            add_words(value_table, WORDS - 1, first, v[:, piece], v_piece[:])
            nc.vector.tensor_tensor(weighted[:, piece], v_piece[:], w[:, piece], MULT)
            stories = range(first // SENTENCES, (first + BANK) // SENTENCES)
            if first + BANK < COLS:
                for b in stories:
                    nc.scalar.activation(unused[:], weighted[:, story(b)], COPY, accum_out=hop2[:, b, 0:1])
            else:
                nc.vector.reduce_sum(
                    hop2[:, stories[0] : STORIES, 0],
                    weighted[:, piece].rearrange("p (b m) -> p b m", m=SENTENCES),
                    axis=X,
                )

        result = held.tile([P, STORIES], F32, name="result")
        nc.vector.tensor_tensor(result[:], hop2[:, :, 0], w_scale[:], MULT)
        nc.vector.tensor_tensor(result[:], result[:], u1[:], ADD)
        nc.sync.dma_start(out, result[:])
